import numpy as np
import ml_dtypes


def mxq(x, axis, fmt="e4m3"):
    dtype, down = {"e4m3": (ml_dtypes.float8_e4m3fn, 7), "e5m2": (ml_dtypes.float8_e5m2, 14)}[fmt]
    v = np.moveaxis(np.asarray(x, np.float32).astype(ml_dtypes.bfloat16).astype(np.float64), axis, -1)
    blocks = v.reshape(v.shape[:-1] + (-1, 32))
    amax = np.abs(blocks).max(-1, keepdims=True)
    byte = np.maximum(np.where(amax > 0, np.frexp(amax)[1] - 1 + 127, 0) - down, 1)
    scale = np.exp2(byte - 127.0)
    codes = (blocks / scale).astype(np.float32).astype(dtype).astype(np.float64)
    return np.moveaxis((codes * scale).reshape(v.shape), -1, axis)


WIDE = False


def mx_kscale(k):
    if not WIDE:
        return np.ones(k)
    levels = np.array([10, -10, 5, -5, 0])
    a = np.random.permutation(np.resize(levels, k // 512 * 4)).reshape(k // 512, 4)
    idx = np.arange(k)
    return np.exp2(a[idx // 512, idx % 128 // 32])


BF16 = ml_dtypes.bfloat16


def bf(x):
    return np.asarray(x, np.float32).astype(BF16)


def f64(x):
    return np.asarray(x).astype(np.float64)


E2M1 = np.array([0.0, 0.5, 1.0, 1.5, 2.0, 3.0, 4.0, 6.0, -0.0, -0.5, -1.0, -1.5, -2.0, -3.0, -4.0, -6.0])


def pack_weight(w, fmt):
    k, n = w.shape
    w = f64(bf(w)).reshape(k // 32, 32, n)
    amax = np.abs(w).max(1)
    if fmt == "e4m3":
        byte = np.frexp(amax)[1] - 1 + 127 - 7
    else:
        mant, ex = np.frexp(amax / 6.0)
        byte = np.where(mant > 0.5, ex, ex - 1) + 127
    byte = np.clip(np.where(amax > 0, byte, 1), 1, 254)
    scaled = (w * np.exp2(127.0 - byte)[:, None, :]).reshape(k, n).astype(np.float32)
    by_word = np.ascontiguousarray(scaled.reshape(k // 512, 128, 4, n).transpose(0, 1, 3, 2))
    if fmt == "e4m3":
        words = by_word.astype(ml_dtypes.float8_e4m3fn).view(np.uint8)
    else:
        c = by_word.astype(ml_dtypes.float4_e2m1fn).view(np.uint8) & 0xF
        words = c[..., 0::2] | (c[..., 1::2] << 4)
    return np.ascontiguousarray(words), np.ascontiguousarray(byte.astype(np.uint8).reshape(k // 512, 16, n))


def unpack_weight(words, scales, fmt):
    g, p, n, _ = words.shape
    if fmt == "e4m3":
        vals = np.ascontiguousarray(words).view(ml_dtypes.float8_e4m3fn).astype(np.float64)
    else:
        nib = np.empty((g, p, n, 4), np.uint8)
        nib[..., 0::2] = words & 0xF
        nib[..., 1::2] = words >> 4
        vals = E2M1[nib]
    vals = vals * np.repeat(np.exp2(scales.astype(np.float64) - 127.0), 8, axis=1)[..., None]
    return vals.transpose(0, 1, 3, 2).reshape(g * 512, n)


B, D_IN, D_OUT = 4096, 512, 512
FMT = "e4m3"


def sigmoid(v):
    return 1.0 / (1.0 + np.exp(-v))


def setup_inputs():
    s, t = mx_kscale(D_IN), mx_kscale(D_OUT)

    def wx():
        return pack_weight(np.random.standard_normal((D_IN, D_OUT)) / np.sqrt(D_IN) / s[:, None], FMT)

    def wh():
        return pack_weight(np.random.standard_normal((D_OUT, D_OUT)) / np.sqrt(D_OUT) / t[:, None], FMT)

    x = bf(np.random.standard_normal((B, D_IN)) * s)
    hist = bf(np.random.standard_normal((B, D_OUT)) * t)
    Wix_words, Wix_scales = wx()
    Wih_words, Wih_scales = wh()
    b_i = bf(np.random.standard_normal(D_OUT) * 0.3)
    Wcx_words, Wcx_scales = wx()
    Wch_words, Wch_scales = wh()
    b_c = bf(np.random.standard_normal(D_OUT) * 0.3)
    return {"x": x,
            "hist": hist,
            "Wix_words": Wix_words, "Wix_scales": Wix_scales,
            "Wih_words": Wih_words, "Wih_scales": Wih_scales,
            "b_i": b_i,
            "Wcx_words": Wcx_words, "Wcx_scales": Wcx_scales,
            "Wch_words": Wch_words, "Wch_scales": Wch_scales,
            "b_c": b_c}


def reference(x, hist, Wix_words, Wix_scales, Wih_words, Wih_scales, b_i, Wcx_words, Wcx_scales, Wch_words, Wch_scales, b_c):
    xq = mxq(f64(x), 1, "e4m3")
    hq = mxq(f64(hist), 1, "e4m3")
    i = sigmoid((xq @ unpack_weight(Wix_words, Wix_scales, FMT)) + (hq @ unpack_weight(Wih_words, Wih_scales, FMT)) + f64(b_i))
    g = np.tanh((xq @ unpack_weight(Wcx_words, Wcx_scales, FMT)) + (hq @ unpack_weight(Wch_words, Wch_scales, FMT)) + f64(b_c))
    return i * g

@@ -1,0 +1,154 @@
+from contextlib import ExitStack
+
+import concourse.mybir as mybir
+from concourse.masks import make_identity
+
+BF16 = mybir.dt.bfloat16
+F32 = mybir.dt.float32
+I32 = mybir.dt.int32
+U32 = mybir.dt.uint32
+U8 = mybir.dt.uint8
+FP8X4 = mybir.dt.float8_e4m3fn_x4
+ACT = mybir.ActivationFunctionType
+ALU = mybir.AluOpType
+
+P = 128
+PACK = 4
+HALVES = 2
+BATCH = 4096
+D = 512
+BLOCKS = BATCH // P
+CHUNK = 4
+CHUNKS = BLOCKS // CHUNK
+K_BLOCKS = D // 32
+QUADRANT = 32
+SCALE_ROWS = 4
+PSUM_BANKS = 8
+
+FLOPS = 4 * 2 * BATCH * D * D
+
+
+def tile_lstmmirrored_pa_t_kernel(
+    tc, x, hist, Wix_words, Wix_scales, Wih_words, Wih_scales, b_i,
+    Wcx_words, Wcx_scales, Wch_words, Wch_scales, b_c, out,
+):
+    nc = tc.nc
+
+    x_blocks = x.rearrange("(p j) k -> p j k", j=BLOCKS)
+    h_blocks = hist.rearrange("(p j) k -> p j k", j=BLOCKS)
+    out_blocks = out.rearrange("(p j) n -> p j n", j=BLOCKS)
+
+    weight_inputs = (
+        (Wix_words, Wix_scales), (Wih_words, Wih_scales),
+        (Wcx_words, Wcx_scales), (Wch_words, Wch_scales),
+    )
+    n_weights = len(weight_inputs)
+
+    with ExitStack() as ctx:
+        consts = ctx.enter_context(tc.tile_pool(name="consts", bufs=1))
+        rows = ctx.enter_context(tc.tile_pool(name="rows", bufs=CHUNKS))
+        quantised = ctx.enter_context(tc.tile_pool(name="quantised", bufs=CHUNKS))
+        stage = ctx.enter_context(tc.tile_pool(name="stage", bufs=4))
+        psum = ctx.enter_context(tc.psum_pool(name="psum", bufs=PSUM_BANKS))
+        ctx.enter_context(tc.manual_schedule())
+
+        w_planes = consts.tile([P, n_weights, D], U8, align_bytes=64)
+        nc.vector.memset(w_planes[:].bitcast(I32), 0)
+        w_words = consts.tile([P, n_weights, D], U32, align_bytes=64)
+
+        bias_rows = consts.tile([P, 2, D], BF16)
+        nc.vector.memset(bias_rows[:], 0.0)
+        ones = consts.tile([P, P], BF16)
+        nc.vector.memset(ones[:], 1.0)
+        nc.scalar.dma_start(out=bias_rows[0:1, 0, :], in_=b_i.rearrange("(o n) -> o n", o=1))
+        nc.scalar.dma_start(out=bias_rows[0:1, 1, :], in_=b_c.rearrange("(o n) -> o n", o=1))
+
+        warm = consts.tile([P, 2], F32)
+        nc.vector.memset(warm[:], 0.0)
+        nc.scalar.activation(out=warm[:, 1:2], in_=warm[:, 0:1], func=ACT.Sigmoid)
+
+        ident = consts.tile([P, P], F32)
+        make_identity(nc, ident[:])
+
+        for w in range(n_weights):
+            scale_rows = weight_inputs[w][1].rearrange("g q n -> (g q) n")
+            for r in range(SCALE_ROWS):
+                nc.gpsimd.dma_start(
+                    out=w_planes[r:P:QUADRANT, w, :].bitcast(F32),
+                    in_=scale_rows[r:K_BLOCKS:SCALE_ROWS, :].bitcast(F32),
+                )
+
+        x_rows = []
+        h_rows = []
+        for c in range(CHUNKS):
+            blocks = slice(c * CHUNK, (c + 1) * CHUNK)
+            x_chunk = rows.tile([P, CHUNK, D], BF16, name="x_chunk")
+            nc.sync.dma_start(out=x_chunk[:], in_=x_blocks[:, blocks, :])
+            h_chunk = rows.tile([P, CHUNK, D], BF16, name="h_chunk")
+            nc.sync.dma_start(out=h_chunk[:], in_=h_blocks[:, blocks, :])
+            x_rows.append(x_chunk)
+            h_rows.append(h_chunk)
+        for w in range(n_weights):
+            nc.sync.dma_start(
+                out=w_words[:, w, :].bitcast(I32),
+                in_=weight_inputs[w][0].rearrange("g p n t -> (g p) (n t)").bitcast(I32),
+            )
+
+        bias = consts.tile([P, 2, D], F32)
+        for gate in range(2):
+            spread = psum.tile([P, D], F32, tag="bank")
+            nc.tensor.matmul(out=spread[:], lhsT=ones[:], rhs=bias_rows[:, gate, :], start=True, stop=True)
+            nc.vector.tensor_copy(out=bias[:, gate, :], in_=spread[:])
+
+        codes = []
+        planes = []
+        for c in range(CHUNKS):
+            chunk_codes = quantised.tile([P, CHUNK, 2, P], U32, align_bytes=64, name="chunk_codes")
+            chunk_planes = quantised.tile([P, CHUNK, 2, P], U8, align_bytes=64, name="chunk_planes")
+            codes.append(chunk_codes)
+            planes.append(chunk_planes)
+            for j in range(CHUNK):
+                flipped = psum.tile([P, 2, HALVES, P], F32, tag="bank")
+                for operand, chunk in enumerate((x_rows[c], h_rows[c])):
+                    pairs = chunk[:, j, :].bitcast(F32)
+                    for u in range(HALVES):
+                        nc.tensor.transpose(
+                            out=flipped[:, operand, u, :], in_=pairs[:, u:D // 2:HALVES], identity=ident[:]
+                        )
+                grouped = stage.tile([P, 2 * P * PACK], BF16, align_bytes=64)
+                grouped_pairs = grouped[:].bitcast(F32).rearrange("p (o r u) -> p o r u", o=2, u=HALVES)
+                flipped_pairs = flipped[:].rearrange("p o u r -> p o r u")
+                if j == 0:
+                    nc.vector.tensor_copy(out=grouped_pairs, in_=flipped_pairs)
+                else:
+                    nc.scalar.copy(out=grouped_pairs, in_=flipped_pairs)
+                nc.vector.quantize_mx(
+                    out=chunk_codes[:, j, :, :].rearrange("p o r -> p (o r)").bitcast(FP8X4),
+                    scales=chunk_planes[:, j, :, :].rearrange("p o r -> p (o r)"),
+                    in_=grouped[:],
+                )
+
+        for b in range(BLOCKS):
+            c, j = divmod(b, CHUNK)
+            gates = []
+            for gate, func in enumerate((ACT.Sigmoid, ACT.Tanh)):
+                acc = psum.tile([P, D], F32, tag="bank")
+                for operand in range(2):
+                    w = 2 * gate + operand
+                    nc.tensor.matmul_mx(
+                        out=acc[:],
+                        lhsT=codes[c][:, j, operand, :].bitcast(FP8X4),
+                        lhsT_scale=planes[c][:, j, operand, :],
+                        rhs=w_words[:, w, :].bitcast(FP8X4),
+                        rhs_scale=w_planes[:, w, :],
+                        start=(operand == 0),
+                        stop=(operand == 1),
+                    )
+                biased = stage.tile([P, D], F32, name="biased%d" % gate)
+                nc.vector.tensor_tensor(out=biased[:], in0=acc[:], in1=bias[:, gate, :], op=ALU.add)
+                squashed = stage.tile([P, D], F32, name="squashed%d" % gate)
+                nc.scalar.activation(out=squashed[:], in_=biased[:], func=func)
+                gates.append(squashed)
+            result = stage.tile([P, D], F32)
+            nc.gpsimd.tensor_tensor(out=result[:], in0=gates[0][:], in1=gates[1][:], op=ALU.mult)
+            nc.sync.dma_start(out=out_blocks[:, b, :], in_=result[:])

@@ -20,6 +20,7 @@ D = 512
 BLOCKS = BATCH // P
 CHUNK = 4
 CHUNKS = BLOCKS // CHUNK
+LAG = 4
 K_BLOCKS = D // 32
 QUADRANT = 32
 SCALE_ROWS = 4
@@ -81,30 +82,26 @@ def tile_lstmmirrored_pa_t_kernel(
         x_rows = []
         h_rows = []
         for c in range(CHUNKS):
+            if c == LAG:
+                for w in range(n_weights):
+                    nc.sync.dma_start(
+                        out=w_words[:, w, :].bitcast(I32),
+                        in_=weight_inputs[w][0].rearrange("g p n t -> (g p) (n t)").bitcast(I32),
+                    )
             blocks = slice(c * CHUNK, (c + 1) * CHUNK)
-            x_chunk = rows.tile([P, CHUNK, D], BF16, name="x_chunk")
+            x_chunk = rows.tile([P, CHUNK, D], BF16)
             nc.sync.dma_start(out=x_chunk[:], in_=x_blocks[:, blocks, :])
-            h_chunk = rows.tile([P, CHUNK, D], BF16, name="h_chunk")
+            h_chunk = rows.tile([P, CHUNK, D], BF16)
             nc.sync.dma_start(out=h_chunk[:], in_=h_blocks[:, blocks, :])
             x_rows.append(x_chunk)
             h_rows.append(h_chunk)
-        for w in range(n_weights):
-            nc.sync.dma_start(
-                out=w_words[:, w, :].bitcast(I32),
-                in_=weight_inputs[w][0].rearrange("g p n t -> (g p) (n t)").bitcast(I32),
-            )
-
-        bias = consts.tile([P, 2, D], F32)
-        for gate in range(2):
-            spread = psum.tile([P, D], F32, tag="bank")
-            nc.tensor.matmul(out=spread[:], lhsT=ones[:], rhs=bias_rows[:, gate, :], start=True, stop=True)
-            nc.vector.tensor_copy(out=bias[:, gate, :], in_=spread[:])
 
         codes = []
         planes = []
-        for c in range(CHUNKS):
-            chunk_codes = quantised.tile([P, CHUNK, 2, P], U32, align_bytes=64, name="chunk_codes")
-            chunk_planes = quantised.tile([P, CHUNK, 2, P], U8, align_bytes=64, name="chunk_planes")
+
+        def stage_1(c):
+            chunk_codes = quantised.tile([P, CHUNK, 2, P], U32, align_bytes=64)
+            chunk_planes = quantised.tile([P, CHUNK, 2, P], U8, align_bytes=64)
             codes.append(chunk_codes)
             planes.append(chunk_planes)
             for j in range(CHUNK):
@@ -128,27 +125,44 @@ def tile_lstmmirrored_pa_t_kernel(
                     in_=grouped[:],
                 )
 
-        for b in range(BLOCKS):
-            c, j = divmod(b, CHUNK)
-            gates = []
-            for gate, func in enumerate((ACT.Sigmoid, ACT.Tanh)):
-                acc = psum.tile([P, D], F32, tag="bank")
-                for operand in range(2):
-                    w = 2 * gate + operand
-                    nc.tensor.matmul_mx(
-                        out=acc[:],
-                        lhsT=codes[c][:, j, operand, :].bitcast(FP8X4),
-                        lhsT_scale=planes[c][:, j, operand, :],
-                        rhs=w_words[:, w, :].bitcast(FP8X4),
-                        rhs_scale=w_planes[:, w, :],
-                        start=(operand == 0),
-                        stop=(operand == 1),
-                    )
-                biased = stage.tile([P, D], F32, name="biased%d" % gate)
-                nc.vector.tensor_tensor(out=biased[:], in0=acc[:], in1=bias[:, gate, :], op=ALU.add)
-                squashed = stage.tile([P, D], F32, name="squashed%d" % gate)
-                nc.scalar.activation(out=squashed[:], in_=biased[:], func=func)
-                gates.append(squashed)
-            result = stage.tile([P, D], F32)
-            nc.gpsimd.tensor_tensor(out=result[:], in0=gates[0][:], in1=gates[1][:], op=ALU.mult)
-            nc.sync.dma_start(out=out_blocks[:, b, :], in_=result[:])
+        bias = consts.tile([P, 2, D], F32)
+
+        def spread_biases():
+            for gate in range(2):
+                spread = psum.tile([P, D], F32, tag="bank")
+                nc.tensor.matmul(out=spread[:], lhsT=ones[:], rhs=bias_rows[:, gate, :], start=True, stop=True)
+                nc.scalar.copy(out=bias[:, gate, :], in_=spread[:])
+
+        def stage_2(c):
+            for j in range(CHUNK):
+                gates = []
+                for gate, func in enumerate((ACT.Sigmoid, ACT.Tanh)):
+                    acc = psum.tile([P, D], F32, tag="bank")
+                    for operand in range(2):
+                        w = 2 * gate + operand
+                        nc.tensor.matmul_mx(
+                            out=acc[:],
+                            lhsT=codes[c][:, j, operand, :].bitcast(FP8X4),
+                            lhsT_scale=planes[c][:, j, operand, :],
+                            rhs=w_words[:, w, :].bitcast(FP8X4),
+                            rhs_scale=w_planes[:, w, :],
+                            start=(operand == 0),
+                            stop=(operand == 1),
+                        )
+                    biased = stage.tile([P, D], F32, name="biased%d" % gate)
+                    nc.vector.tensor_tensor(out=biased[:], in0=acc[:], in1=bias[:, gate, :], op=ALU.add)
+                    squashed = stage.tile([P, D], F32, name="squashed%d" % gate)
+                    nc.scalar.activation(out=squashed[:], in_=biased[:], func=func)
+                    gates.append(squashed)
+                result = stage.tile([P, D], F32)
+                nc.gpsimd.tensor_tensor(out=result[:], in0=gates[0][:], in1=gates[1][:], op=ALU.mult)
+                nc.sync.dma_start(out=out_blocks[:, c * CHUNK + j, :], in_=result[:])
+
+        for c in range(LAG):
+            stage_1(c)
+        spread_biases()
+        for c in range(LAG, CHUNKS):
+            stage_1(c)
+            stage_2(c - LAG)
+        for c in range(CHUNKS - LAG, CHUNKS):
+            stage_2(c)

@@ -20,7 +20,8 @@ D = 512
 BLOCKS = BATCH // P
 CHUNK = 4
 CHUNKS = BLOCKS // CHUNK
-LAG = 4
+BEHIND = 2
+VECTOR_TURN = 8
 K_BLOCKS = D // 32
 QUADRANT = 32
 SCALE_ROWS = 4
@@ -49,7 +50,7 @@ def tile_lstmmirrored_pa_t_kernel(
         consts = ctx.enter_context(tc.tile_pool(name="consts", bufs=1))
         rows = ctx.enter_context(tc.tile_pool(name="rows", bufs=CHUNKS))
         quantised = ctx.enter_context(tc.tile_pool(name="quantised", bufs=CHUNKS))
-        stage = ctx.enter_context(tc.tile_pool(name="stage", bufs=4))
+        stage = ctx.enter_context(tc.tile_pool(name="stage", bufs=6))
         psum = ctx.enter_context(tc.psum_pool(name="psum", bufs=PSUM_BANKS))
         ctx.enter_context(tc.manual_schedule())
 
@@ -81,13 +82,8 @@ def tile_lstmmirrored_pa_t_kernel(
 
         x_rows = []
         h_rows = []
-        for c in range(CHUNKS):
-            if c == LAG:
-                for w in range(n_weights):
-                    nc.sync.dma_start(
-                        out=w_words[:, w, :].bitcast(I32),
-                        in_=weight_inputs[w][0].rearrange("g p n t -> (g p) (n t)").bitcast(I32),
-                    )
+
+        def load_chunk(c):
             blocks = slice(c * CHUNK, (c + 1) * CHUNK)
             x_chunk = rows.tile([P, CHUNK, D], BF16)
             nc.sync.dma_start(out=x_chunk[:], in_=x_blocks[:, blocks, :])
@@ -95,6 +91,14 @@ def tile_lstmmirrored_pa_t_kernel(
             nc.sync.dma_start(out=h_chunk[:], in_=h_blocks[:, blocks, :])
             x_rows.append(x_chunk)
             h_rows.append(h_chunk)
+
+        for c in range(CHUNKS):
+            load_chunk(c)
+        for w in range(n_weights):
+            nc.sync.dma_start(
+                out=w_words[:, w, :].bitcast(I32),
+                in_=weight_inputs[w][0].rearrange("g p n t -> (g p) (n t)").bitcast(I32),
+            )
 
         codes = []
         planes = []
@@ -133,36 +137,40 @@ def tile_lstmmirrored_pa_t_kernel(
                 nc.tensor.matmul(out=spread[:], lhsT=ones[:], rhs=bias_rows[:, gate, :], start=True, stop=True)
                 nc.scalar.copy(out=bias[:, gate, :], in_=spread[:])
 
-        def stage_2(c):
-            for j in range(CHUNK):
-                gates = []
-                for gate, func in enumerate((ACT.Sigmoid, ACT.Tanh)):
-                    acc = psum.tile([P, D], F32, tag="bank")
-                    for operand in range(2):
-                        w = 2 * gate + operand
-                        nc.tensor.matmul_mx(
-                            out=acc[:],
-                            lhsT=codes[c][:, j, operand, :].bitcast(FP8X4),
-                            lhsT_scale=planes[c][:, j, operand, :],
-                            rhs=w_words[:, w, :].bitcast(FP8X4),
-                            rhs_scale=w_planes[:, w, :],
-                            start=(operand == 0),
-                            stop=(operand == 1),
-                        )
-                    biased = stage.tile([P, D], F32, name="biased%d" % gate)
-                    nc.vector.tensor_tensor(out=biased[:], in0=acc[:], in1=bias[:, gate, :], op=ALU.add)
-                    squashed = stage.tile([P, D], F32, name="squashed%d" % gate)
-                    nc.scalar.activation(out=squashed[:], in_=biased[:], func=func)
-                    gates.append(squashed)
-                result = stage.tile([P, D], F32)
-                nc.gpsimd.tensor_tensor(out=result[:], in0=gates[0][:], in1=gates[1][:], op=ALU.mult)
-                nc.sync.dma_start(out=out_blocks[:, c * CHUNK + j, :], in_=result[:])
+        gates = []
 
-        for c in range(LAG):
+        def squash(b):
+            c, j = divmod(b, CHUNK)
+            for gate, func in enumerate((ACT.Sigmoid, ACT.Tanh)):
+                acc = psum.tile([P, D], F32, tag="bank")
+                for operand in range(2):
+                    w = 2 * gate + operand
+                    nc.tensor.matmul_mx(
+                        out=acc[:],
+                        lhsT=codes[c][:, j, operand, :].bitcast(FP8X4),
+                        lhsT_scale=planes[c][:, j, operand, :],
+                        rhs=w_words[:, w, :].bitcast(FP8X4),
+                        rhs_scale=w_planes[:, w, :],
+                        start=(operand == 0),
+                        stop=(operand == 1),
+                    )
+                biased = stage.tile([P, D], F32, name="biased%d" % gate)
+                nc.vector.tensor_tensor(out=biased[:], in0=acc[:], in1=bias[:, gate, :], op=ALU.add)
+                squashed = stage.tile([P, D], F32, name="squashed%d" % gate)
+                nc.scalar.activation(out=squashed[:], in_=biased[:], func=func)
+                gates.append(squashed)
+
+        def multiply(b):
+            result = stage.tile([P, D], F32)
+            multiplier = nc.vector if b % VECTOR_TURN == VECTOR_TURN - 1 else nc.gpsimd
+            multiplier.tensor_tensor(out=result[:], in0=gates[2 * b][:], in1=gates[2 * b + 1][:], op=ALU.mult)
+            nc.sync.dma_start(out=out_blocks[:, b, :], in_=result[:])
+
+        for c in range(CHUNKS):
             stage_1(c)
         spread_biases()
-        for c in range(LAG, CHUNKS):
-            stage_1(c)
-            stage_2(c - LAG)
-        for c in range(CHUNKS - LAG, CHUNKS):
-            stage_2(c)
+        for b in range(BLOCKS + BEHIND):
+            if b < BLOCKS:
+                squash(b)
+            if b >= BEHIND:
+                multiply(b - BEHIND)

@@ -21,7 +21,7 @@ BLOCKS = BATCH // P
 CHUNK = 4
 CHUNKS = BLOCKS // CHUNK
 BEHIND = 2
-VECTOR_TURN = 8
+VECTOR_TURN = 64
 K_BLOCKS = D // 32
 QUADRANT = 32
 SCALE_ROWS = 4

@@ -21,7 +21,7 @@ BLOCKS = BATCH // P
 CHUNK = 4
 CHUNKS = BLOCKS // CHUNK
 BEHIND = 2
-VECTOR_TURN = 64
+VECTOR_TURN = 8
 K_BLOCKS = D // 32
 QUADRANT = 32
 SCALE_ROWS = 4
@@ -72,14 +72,6 @@ def tile_lstmmirrored_pa_t_kernel(
         ident = consts.tile([P, P], F32)
         make_identity(nc, ident[:])
 
-        for w in range(n_weights):
-            scale_rows = weight_inputs[w][1].rearrange("g q n -> (g q) n")
-            for r in range(SCALE_ROWS):
-                nc.gpsimd.dma_start(
-                    out=w_planes[r:P:QUADRANT, w, :].bitcast(F32),
-                    in_=scale_rows[r:K_BLOCKS:SCALE_ROWS, :].bitcast(F32),
-                )
-
         x_rows = []
         h_rows = []
 
@@ -92,8 +84,18 @@ def tile_lstmmirrored_pa_t_kernel(
             x_rows.append(x_chunk)
             h_rows.append(h_chunk)
 
+        def load_scale_rows(w):
+            scale_rows = weight_inputs[w][1].rearrange("g q n -> (g q) n")
+            for r in range(SCALE_ROWS):
+                nc.sync.dma_start(
+                    out=w_planes[r:P:QUADRANT, w, :].bitcast(I32),
+                    in_=scale_rows[r:K_BLOCKS:SCALE_ROWS, :].bitcast(I32),
+                )
+
         for c in range(CHUNKS):
             load_chunk(c)
+            if c < n_weights:
+                load_scale_rows(c)
         for w in range(n_weights):
             nc.sync.dma_start(
                 out=w_words[:, w, :].bitcast(I32),

@@ -20,8 +20,8 @@ D = 512
 BLOCKS = BATCH // P
 CHUNK = 4
 CHUNKS = BLOCKS // CHUNK
-BEHIND = 2
-VECTOR_TURN = 8
+PAIR = 2
+VECTOR_LAST = 4
 K_BLOCKS = D // 32
 QUADRANT = 32
 SCALE_ROWS = 4
@@ -51,6 +51,7 @@ def tile_lstmmirrored_pa_t_kernel(
         rows = ctx.enter_context(tc.tile_pool(name="rows", bufs=CHUNKS))
         quantised = ctx.enter_context(tc.tile_pool(name="quantised", bufs=CHUNKS))
         stage = ctx.enter_context(tc.tile_pool(name="stage", bufs=6))
+        pairs_pool = ctx.enter_context(tc.tile_pool(name="pairs", bufs=4))
         psum = ctx.enter_context(tc.psum_pool(name="psum", bufs=PSUM_BANKS))
         ctx.enter_context(tc.manual_schedule())
 
@@ -143,6 +144,10 @@ def tile_lstmmirrored_pa_t_kernel(
 
         def squash(b):
             c, j = divmod(b, CHUNK)
+            if b % PAIR == 0:
+                for gate in range(2):
+                    squashed = pairs_pool.tile([P, PAIR, D], F32, name="squashed%d" % gate)
+                    gates.append(squashed)
             for gate, func in enumerate((ACT.Sigmoid, ACT.Tanh)):
                 acc = psum.tile([P, D], F32, tag="bank")
                 for operand in range(2):
@@ -158,21 +163,25 @@ def tile_lstmmirrored_pa_t_kernel(
                     )
                 biased = stage.tile([P, D], F32, name="biased%d" % gate)
                 nc.vector.tensor_tensor(out=biased[:], in0=acc[:], in1=bias[:, gate, :], op=ALU.add)
-                squashed = stage.tile([P, D], F32, name="squashed%d" % gate)
-                nc.scalar.activation(out=squashed[:], in_=biased[:], func=func)
-                gates.append(squashed)
+                nc.scalar.activation(out=gates[2 * (b // PAIR) + gate][:, b % PAIR, :], in_=biased[:], func=func)
 
-        def multiply(b):
-            result = stage.tile([P, D], F32)
-            multiplier = nc.vector if b % VECTOR_TURN == VECTOR_TURN - 1 else nc.gpsimd
-            multiplier.tensor_tensor(out=result[:], in0=gates[2 * b][:], in1=gates[2 * b + 1][:], op=ALU.mult)
-            nc.sync.dma_start(out=out_blocks[:, b, :], in_=result[:])
+        def multiply(first, count, multiplier):
+            halves = slice(first % PAIR, first % PAIR + count)
+            result = pairs_pool.tile([P, PAIR, D], F32)
+            multiplier.tensor_tensor(
+                out=result[:, halves, :],
+                in0=gates[2 * (first // PAIR)][:, halves, :],
+                in1=gates[2 * (first // PAIR) + 1][:, halves, :],
+                op=ALU.mult,
+            )
+            nc.sync.dma_start(out=out_blocks[:, first:first + count, :], in_=result[:, halves, :])
 
         for c in range(CHUNKS):
             stage_1(c)
         spread_biases()
-        for b in range(BLOCKS + BEHIND):
-            if b < BLOCKS:
-                squash(b)
-            if b >= BEHIND:
-                multiply(b - BEHIND)
+        for b in range(BLOCKS):
+            squash(b)
+            if b % PAIR == PAIR - 1 and b < BLOCKS - VECTOR_LAST:
+                multiply(b - PAIR + 1, PAIR, nc.gpsimd)
+        for b in range(BLOCKS - VECTOR_LAST, BLOCKS):
+            multiply(b, 1, nc.vector)

@@ -52,6 +52,8 @@ def tile_lstmmirrored_pa_t_kernel(
         quantised = ctx.enter_context(tc.tile_pool(name="quantised", bufs=CHUNKS))
         stage = ctx.enter_context(tc.tile_pool(name="stage", bufs=6))
         pairs_pool = ctx.enter_context(tc.tile_pool(name="pairs", bufs=4))
+        sums_pool = ctx.enter_context(tc.tile_pool(name="sums", bufs=3))
+        results = ctx.enter_context(tc.tile_pool(name="results", bufs=8))
         psum = ctx.enter_context(tc.psum_pool(name="psum", bufs=PSUM_BANKS))
         ctx.enter_context(tc.manual_schedule())
 
@@ -141,6 +143,7 @@ def tile_lstmmirrored_pa_t_kernel(
                 nc.scalar.copy(out=bias[:, gate, :], in_=spread[:])
 
         gates = []
+        biased_pairs = []
 
         def squash(b):
             c, j = divmod(b, CHUNK)
@@ -148,6 +151,8 @@ def tile_lstmmirrored_pa_t_kernel(
                 for gate in range(2):
                     squashed = pairs_pool.tile([P, PAIR, D], F32, name="squashed%d" % gate)
                     gates.append(squashed)
+                biased_pair = sums_pool.tile([P, PAIR, 2, D], F32)
+                biased_pairs.append(biased_pair)
             for gate, func in enumerate((ACT.Sigmoid, ACT.Tanh)):
                 acc = psum.tile([P, D], F32, tag="bank")
                 for operand in range(2):
@@ -161,20 +166,20 @@ def tile_lstmmirrored_pa_t_kernel(
                         start=(operand == 0),
                         stop=(operand == 1),
                     )
-                biased = stage.tile([P, D], F32, name="biased%d" % gate)
-                nc.vector.tensor_tensor(out=biased[:], in0=acc[:], in1=bias[:, gate, :], op=ALU.add)
-                nc.scalar.activation(out=gates[2 * (b // PAIR) + gate][:, b % PAIR, :], in_=biased[:], func=func)
+                biased = biased_pairs[b // PAIR][:, b % PAIR, gate, :]
+                nc.vector.tensor_tensor(out=biased, in0=acc[:], in1=bias[:, gate, :], op=ALU.add)
+                nc.scalar.activation(out=gates[2 * (b // PAIR) + gate][:, b % PAIR, :], in_=biased, func=func)
 
-        def multiply(first, count, multiplier):
+        def multiply(first, count, multiplier, queue):
             halves = slice(first % PAIR, first % PAIR + count)
-            result = pairs_pool.tile([P, PAIR, D], F32)
+            result = results.tile([P, PAIR, D], F32)
             multiplier.tensor_tensor(
                 out=result[:, halves, :],
                 in0=gates[2 * (first // PAIR)][:, halves, :],
                 in1=gates[2 * (first // PAIR) + 1][:, halves, :],
                 op=ALU.mult,
             )
-            nc.sync.dma_start(out=out_blocks[:, first:first + count, :], in_=result[:, halves, :])
+            queue.dma_start(out=out_blocks[:, first:first + count, :], in_=result[:, halves, :])
 
         for c in range(CHUNKS):
             stage_1(c)
@@ -182,6 +187,6 @@ def tile_lstmmirrored_pa_t_kernel(
         for b in range(BLOCKS):
             squash(b)
             if b % PAIR == PAIR - 1 and b < BLOCKS - VECTOR_LAST:
-                multiply(b - PAIR + 1, PAIR, nc.gpsimd)
+                multiply(b - PAIR + 1, PAIR, nc.gpsimd, nc.sync)
         for b in range(BLOCKS - VECTOR_LAST, BLOCKS):
-            multiply(b, 1, nc.vector)
+            multiply(b, 1, nc.vector, nc.scalar)

@@ -78,27 +78,27 @@ def tile_lstmmirrored_pa_t_kernel(
         x_rows = []
         h_rows = []
 
+        def load_scale_rows(turn):
+            w, r = divmod(turn, SCALE_ROWS)
+            scale_rows = weight_inputs[w][1].rearrange("g q n -> (g q) n")
+            nc.sync.dma_start(
+                out=w_planes[r:P:QUADRANT, w, :].bitcast(I32),
+                in_=scale_rows[r:K_BLOCKS:SCALE_ROWS, :].bitcast(I32),
+            )
+
         def load_chunk(c):
             blocks = slice(c * CHUNK, (c + 1) * CHUNK)
             x_chunk = rows.tile([P, CHUNK, D], BF16)
             nc.sync.dma_start(out=x_chunk[:], in_=x_blocks[:, blocks, :])
+            load_scale_rows(2 * c)
             h_chunk = rows.tile([P, CHUNK, D], BF16)
             nc.sync.dma_start(out=h_chunk[:], in_=h_blocks[:, blocks, :])
+            load_scale_rows(2 * c + 1)
             x_rows.append(x_chunk)
             h_rows.append(h_chunk)
 
-        def load_scale_rows(w):
-            scale_rows = weight_inputs[w][1].rearrange("g q n -> (g q) n")
-            for r in range(SCALE_ROWS):
-                nc.sync.dma_start(
-                    out=w_planes[r:P:QUADRANT, w, :].bitcast(I32),
-                    in_=scale_rows[r:K_BLOCKS:SCALE_ROWS, :].bitcast(I32),
-                )
-
         for c in range(CHUNKS):
             load_chunk(c)
-            if c < n_weights:
-                load_scale_rows(c)
         for w in range(n_weights):
             nc.sync.dma_start(
                 out=w_words[:, w, :].bitcast(I32),

@@ -21,6 +21,9 @@ BLOCKS = BATCH // P
 CHUNK = 4
 CHUNKS = BLOCKS // CHUNK
 PAIR = 2
+SORTED = 2
+LAG = 2
+BIAS_AFTER = 3
 VECTOR_LAST = 4
 K_BLOCKS = D // 32
 QUADRANT = 32
@@ -50,6 +53,7 @@ def tile_lstmmirrored_pa_t_kernel(
         consts = ctx.enter_context(tc.tile_pool(name="consts", bufs=1))
         rows = ctx.enter_context(tc.tile_pool(name="rows", bufs=CHUNKS))
         quantised = ctx.enter_context(tc.tile_pool(name="quantised", bufs=CHUNKS))
+        sorts = ctx.enter_context(tc.tile_pool(name="sorts", bufs=4))
         stage = ctx.enter_context(tc.tile_pool(name="stage", bufs=6))
         pairs_pool = ctx.enter_context(tc.tile_pool(name="pairs", bufs=4))
         sums_pool = ctx.enter_context(tc.tile_pool(name="sums", bufs=3))
@@ -108,31 +112,49 @@ def tile_lstmmirrored_pa_t_kernel(
         codes = []
         planes = []
 
-        def stage_1(c):
-            chunk_codes = quantised.tile([P, CHUNK, 2, P], U32, align_bytes=64)
-            chunk_planes = quantised.tile([P, CHUNK, 2, P], U8, align_bytes=64)
-            codes.append(chunk_codes)
-            planes.append(chunk_planes)
-            for j in range(CHUNK):
-                flipped = psum.tile([P, 2, HALVES, P], F32, tag="bank")
-                for operand, chunk in enumerate((x_rows[c], h_rows[c])):
-                    pairs = chunk[:, j, :].bitcast(F32)
-                    for u in range(HALVES):
-                        nc.tensor.transpose(
-                            out=flipped[:, operand, u, :], in_=pairs[:, u:D // 2:HALVES], identity=ident[:]
-                        )
-                grouped = stage.tile([P, 2 * P * PACK], BF16, align_bytes=64)
-                grouped_pairs = grouped[:].bitcast(F32).rearrange("p (o r u) -> p o r u", o=2, u=HALVES)
-                flipped_pairs = flipped[:].rearrange("p o u r -> p o r u")
-                if j == 0:
-                    nc.vector.tensor_copy(out=grouped_pairs, in_=flipped_pairs)
-                else:
-                    nc.scalar.copy(out=grouped_pairs, in_=flipped_pairs)
+        waiting = []
+
+        def quantise(leave):
+            while len(waiting) > leave:
+                grouped, chunk_codes, chunk_planes, j = waiting.pop(0)
                 nc.vector.quantize_mx(
                     out=chunk_codes[:, j, :, :].rearrange("p o r -> p (o r)").bitcast(FP8X4),
                     scales=chunk_planes[:, j, :, :].rearrange("p o r -> p (o r)"),
                     in_=grouped[:],
                 )
+
+        def stage_1(c):
+            chunk_codes = quantised.tile([P, CHUNK, 2, P], U32, align_bytes=64)
+            chunk_planes = quantised.tile([P, CHUNK, 2, P], U8, align_bytes=64)
+            codes.append(chunk_codes)
+            planes.append(chunk_planes)
+            sorted_words = []
+            for chunk in (x_rows[c], h_rows[c]):
+                words = sorts.tile([P, SORTED, HALVES, P], F32)
+                nc.vector.tensor_copy(
+                    out=words[:],
+                    in_=chunk[:, CHUNK - SORTED:, :].rearrange("p j k -> p (j k)").bitcast(F32).rearrange(
+                        "p (j w u) -> p j u w", j=SORTED, u=HALVES
+                    ),
+                )
+                sorted_words.append(words)
+            for j in range(CHUNK):
+                flipped = psum.tile([P, 2, HALVES, P], F32, tag="bank")
+                for operand, chunk in enumerate((x_rows[c], h_rows[c])):
+                    pairs = chunk[:, j, :].bitcast(F32)
+                    for u in range(HALVES):
+                        if j < CHUNK - SORTED:
+                            words = pairs[:, u:D // 2:HALVES]
+                        else:
+                            words = sorted_words[operand][:, j - (CHUNK - SORTED), u, :]
+                        nc.tensor.transpose(out=flipped[:, operand, u, :], in_=words, identity=ident[:])
+                grouped = stage.tile([P, 2 * P * PACK], BF16, align_bytes=64)
+                nc.scalar.copy(
+                    out=grouped[:].bitcast(F32).rearrange("p (o r u) -> p o r u", o=2, u=HALVES),
+                    in_=flipped[:].rearrange("p o u r -> p o r u"),
+                )
+                waiting.append((grouped, chunk_codes, chunk_planes, j))
+                quantise(LAG)
 
         bias = consts.tile([P, 2, D], F32)
 
@@ -183,7 +205,9 @@ def tile_lstmmirrored_pa_t_kernel(
 
         for c in range(CHUNKS):
             stage_1(c)
-        spread_biases()
+            if c == BIAS_AFTER:
+                spread_biases()
+        quantise(0)
         for b in range(BLOCKS):
             squash(b)
             if b % PAIR == PAIR - 1 and b < BLOCKS - VECTOR_LAST:

@@ -21,9 +21,10 @@ BLOCKS = BATCH // P
 CHUNK = 4
 CHUNKS = BLOCKS // CHUNK
 PAIR = 2
-SORTED = 2
-LAG = 2
+LAG = 4
 BIAS_AFTER = 3
+SINGLES_UNTIL = 4
+SINGLES_FROM = 26
 VECTOR_LAST = 4
 K_BLOCKS = D // 32
 QUADRANT = 32
@@ -51,12 +52,9 @@ def tile_lstmmirrored_pa_t_kernel(
 
     with ExitStack() as ctx:
         consts = ctx.enter_context(tc.tile_pool(name="consts", bufs=1))
-        rows = ctx.enter_context(tc.tile_pool(name="rows", bufs=CHUNKS))
-        quantised = ctx.enter_context(tc.tile_pool(name="quantised", bufs=CHUNKS))
         sorts = ctx.enter_context(tc.tile_pool(name="sorts", bufs=4))
-        stage = ctx.enter_context(tc.tile_pool(name="stage", bufs=6))
-        pairs_pool = ctx.enter_context(tc.tile_pool(name="pairs", bufs=4))
-        sums_pool = ctx.enter_context(tc.tile_pool(name="sums", bufs=3))
+        stage = ctx.enter_context(tc.tile_pool(name="stage", bufs=8))
+        pairs_pool = ctx.enter_context(tc.tile_pool(name="pairs", bufs=6))
         results = ctx.enter_context(tc.tile_pool(name="results", bufs=8))
         psum = ctx.enter_context(tc.psum_pool(name="psum", bufs=PSUM_BANKS))
         ctx.enter_context(tc.manual_schedule())
@@ -79,82 +77,71 @@ def tile_lstmmirrored_pa_t_kernel(
         ident = consts.tile([P, P], F32)
         make_identity(nc, ident[:])
 
-        x_rows = []
-        h_rows = []
+        operands = []
+        for name, blocks in (("x_rows", x_blocks), ("h_rows", h_blocks)):
+            operand_rows = consts.tile([P, BLOCKS, D], BF16, name=name)
+            operands.append((operand_rows, blocks))
+        scale_turns = list(range(n_weights * SCALE_ROWS))
 
-        def load_scale_rows(turn):
-            w, r = divmod(turn, SCALE_ROWS)
+        def load_scale_rows():
+            w, r = divmod(scale_turns.pop(0), SCALE_ROWS)
             scale_rows = weight_inputs[w][1].rearrange("g q n -> (g q) n")
             nc.sync.dma_start(
                 out=w_planes[r:P:QUADRANT, w, :].bitcast(I32),
                 in_=scale_rows[r:K_BLOCKS:SCALE_ROWS, :].bitcast(I32),
             )
 
-        def load_chunk(c):
-            blocks = slice(c * CHUNK, (c + 1) * CHUNK)
-            x_chunk = rows.tile([P, CHUNK, D], BF16)
-            nc.sync.dma_start(out=x_chunk[:], in_=x_blocks[:, blocks, :])
-            load_scale_rows(2 * c)
-            h_chunk = rows.tile([P, CHUNK, D], BF16)
-            nc.sync.dma_start(out=h_chunk[:], in_=h_blocks[:, blocks, :])
-            load_scale_rows(2 * c + 1)
-            x_rows.append(x_chunk)
-            h_rows.append(h_chunk)
-
         for c in range(CHUNKS):
-            load_chunk(c)
+            chunk = slice(c * CHUNK, (c + 1) * CHUNK)
+            for operand_rows, blocks in operands:
+                nc.sync.dma_start(out=operand_rows[:, chunk, :], in_=blocks[:, chunk, :])
+                load_scale_rows()
         for w in range(n_weights):
             nc.sync.dma_start(
                 out=w_words[:, w, :].bitcast(I32),
                 in_=weight_inputs[w][0].rearrange("g p n t -> (g p) (n t)").bitcast(I32),
             )
 
-        codes = []
-        planes = []
-
+        codes = consts.tile([P, 2, BLOCKS, P], U32, align_bytes=64)
+        planes = consts.tile([P, 2, BLOCKS, P], U8, align_bytes=64)
         waiting = []
 
         def quantise(leave):
             while len(waiting) > leave:
-                grouped, chunk_codes, chunk_planes, j = waiting.pop(0)
+                grouped, operand, b = waiting.pop(0)
                 nc.vector.quantize_mx(
-                    out=chunk_codes[:, j, :, :].rearrange("p o r -> p (o r)").bitcast(FP8X4),
-                    scales=chunk_planes[:, j, :, :].rearrange("p o r -> p (o r)"),
+                    out=codes[:, operand, b:b + PAIR, :].rearrange("p j r -> p (j r)").bitcast(FP8X4),
+                    scales=planes[:, operand, b:b + PAIR, :].rearrange("p j r -> p (j r)"),
                     in_=grouped[:],
                 )
 
-        def stage_1(c):
-            chunk_codes = quantised.tile([P, CHUNK, 2, P], U32, align_bytes=64)
-            chunk_planes = quantised.tile([P, CHUNK, 2, P], U8, align_bytes=64)
-            codes.append(chunk_codes)
-            planes.append(chunk_planes)
-            sorted_words = []
-            for chunk in (x_rows[c], h_rows[c]):
-                words = sorts.tile([P, SORTED, HALVES, P], F32)
-                nc.vector.tensor_copy(
-                    out=words[:],
-                    in_=chunk[:, CHUNK - SORTED:, :].rearrange("p j k -> p (j k)").bitcast(F32).rearrange(
-                        "p (j w u) -> p j u w", j=SORTED, u=HALVES
-                    ),
-                )
-                sorted_words.append(words)
-            for j in range(CHUNK):
-                flipped = psum.tile([P, 2, HALVES, P], F32, tag="bank")
-                for operand, chunk in enumerate((x_rows[c], h_rows[c])):
-                    pairs = chunk[:, j, :].bitcast(F32)
-                    for u in range(HALVES):
-                        if j < CHUNK - SORTED:
-                            words = pairs[:, u:D // 2:HALVES]
-                        else:
-                            words = sorted_words[operand][:, j - (CHUNK - SORTED), u, :]
-                        nc.tensor.transpose(out=flipped[:, operand, u, :], in_=words, identity=ident[:])
-                grouped = stage.tile([P, 2 * P * PACK], BF16, align_bytes=64)
-                nc.scalar.copy(
-                    out=grouped[:].bitcast(F32).rearrange("p (o r u) -> p o r u", o=2, u=HALVES),
-                    in_=flipped[:].rearrange("p o u r -> p o r u"),
-                )
-                waiting.append((grouped, chunk_codes, chunk_planes, j))
-                quantise(LAG)
+        def sort_words(operand, b):
+            words = sorts.tile([P, PAIR, HALVES, P], F32)
+            nc.vector.tensor_copy(
+                out=words[:],
+                in_=operands[operand][0][:, b:b + PAIR, :].rearrange("p j k -> p (j k)").bitcast(F32).rearrange(
+                    "p (j w u) -> p j u w", j=PAIR, u=HALVES
+                ),
+            )
+            return words
+
+        def stage_1(operand, b, words):
+            flipped = psum.tile([P, PAIR, HALVES, P], F32, tag="bank")
+            for j in range(PAIR):
+                pairs = operands[operand][0][:, b + j, :].bitcast(F32)
+                for u in range(HALVES):
+                    if words is None:
+                        half = pairs[:, u:D // 2:HALVES]
+                    else:
+                        half = words[:, j, u, :]
+                    nc.tensor.transpose(out=flipped[:, j, u, :], in_=half, identity=ident[:])
+            grouped = stage.tile([P, PAIR * P * PACK], BF16, align_bytes=64)
+            nc.scalar.copy(
+                out=grouped[:].bitcast(F32).rearrange("p (j r u) -> p j r u", j=PAIR, u=HALVES),
+                in_=flipped[:].rearrange("p j u r -> p j r u"),
+            )
+            waiting.append((grouped, operand, b))
+            quantise(LAG)
 
         bias = consts.tile([P, 2, D], F32)
 
@@ -165,32 +152,28 @@ def tile_lstmmirrored_pa_t_kernel(
                 nc.scalar.copy(out=bias[:, gate, :], in_=spread[:])
 
         gates = []
-        biased_pairs = []
 
         def squash(b):
-            c, j = divmod(b, CHUNK)
             if b % PAIR == 0:
                 for gate in range(2):
                     squashed = pairs_pool.tile([P, PAIR, D], F32, name="squashed%d" % gate)
                     gates.append(squashed)
-                biased_pair = sums_pool.tile([P, PAIR, 2, D], F32)
-                biased_pairs.append(biased_pair)
             for gate, func in enumerate((ACT.Sigmoid, ACT.Tanh)):
                 acc = psum.tile([P, D], F32, tag="bank")
                 for operand in range(2):
                     w = 2 * gate + operand
                     nc.tensor.matmul_mx(
                         out=acc[:],
-                        lhsT=codes[c][:, j, operand, :].bitcast(FP8X4),
-                        lhsT_scale=planes[c][:, j, operand, :],
+                        lhsT=codes[:, operand, b, :].bitcast(FP8X4),
+                        lhsT_scale=planes[:, operand, b, :],
                         rhs=w_words[:, w, :].bitcast(FP8X4),
                         rhs_scale=w_planes[:, w, :],
                         start=(operand == 0),
                         stop=(operand == 1),
                     )
-                biased = biased_pairs[b // PAIR][:, b % PAIR, gate, :]
+                biased = gates[2 * (b // PAIR) + gate][:, b % PAIR, :]
                 nc.vector.tensor_tensor(out=biased, in0=acc[:], in1=bias[:, gate, :], op=ALU.add)
-                nc.scalar.activation(out=gates[2 * (b // PAIR) + gate][:, b % PAIR, :], in_=biased, func=func)
+                nc.scalar.activation(out=biased, in_=biased, func=func)
 
         def multiply(first, count, multiplier, queue):
             halves = slice(first % PAIR, first % PAIR + count)
@@ -204,13 +187,19 @@ def tile_lstmmirrored_pa_t_kernel(
             queue.dma_start(out=out_blocks[:, first:first + count, :], in_=result[:, halves, :])
 
         for c in range(CHUNKS):
-            stage_1(c)
+            for operand in range(2):
+                b = c * CHUNK
+                words = sort_words(operand, b + PAIR)
+                stage_1(operand, b, None)
+                stage_1(operand, b + PAIR, words)
             if c == BIAS_AFTER:
                 spread_biases()
         quantise(0)
         for b in range(BLOCKS):
             squash(b)
-            if b % PAIR == PAIR - 1 and b < BLOCKS - VECTOR_LAST:
+            if b < SINGLES_UNTIL or SINGLES_FROM <= b < BLOCKS - VECTOR_LAST:
+                multiply(b, 1, nc.gpsimd, nc.sync)
+            elif b % PAIR == PAIR - 1 and b < SINGLES_FROM:
                 multiply(b - PAIR + 1, PAIR, nc.gpsimd, nc.sync)
         for b in range(BLOCKS - VECTOR_LAST, BLOCKS):
             multiply(b, 1, nc.vector, nc.scalar)

@@ -59,9 +59,9 @@ def tile_lstmmirrored_pa_t_kernel(
         psum = ctx.enter_context(tc.psum_pool(name="psum", bufs=PSUM_BANKS))
         ctx.enter_context(tc.manual_schedule())
 
-        w_planes = consts.tile([P, n_weights, D], U8, align_bytes=64)
+        w_planes = consts.tile([P, n_weights, D], U8, align_bytes=256)
         nc.vector.memset(w_planes[:].bitcast(I32), 0)
-        w_words = consts.tile([P, n_weights, D], U32, align_bytes=64)
+        w_words = consts.tile([P, n_weights, D], U32, align_bytes=256)
 
         bias_rows = consts.tile([P, 2, D], BF16)
         nc.vector.memset(bias_rows[:], 0.0)
@@ -102,8 +102,8 @@ def tile_lstmmirrored_pa_t_kernel(
                 in_=weight_inputs[w][0].rearrange("g p n t -> (g p) (n t)").bitcast(I32),
             )
 
-        codes = consts.tile([P, 2, BLOCKS, P], U32, align_bytes=64)
-        planes = consts.tile([P, 2, BLOCKS, P], U8, align_bytes=64)
+        codes = consts.tile([P, 2, BLOCKS, P], U32, align_bytes=256)
+        planes = consts.tile([P, 2, BLOCKS, P], U8, align_bytes=256)
         waiting = []
 
         def quantise(leave):
@@ -135,7 +135,7 @@ def tile_lstmmirrored_pa_t_kernel(
                     else:
                         half = words[:, j, u, :]
                     nc.tensor.transpose(out=flipped[:, j, u, :], in_=half, identity=ident[:])
-            grouped = stage.tile([P, PAIR * P * PACK], BF16, align_bytes=64)
+            grouped = stage.tile([P, PAIR * P * PACK], BF16, align_bytes=256)
             nc.scalar.copy(
                 out=grouped[:].bitcast(F32).rearrange("p (j r u) -> p j r u", j=PAIR, u=HALVES),
                 in_=flipped[:].rearrange("p j u r -> p j r u"),

@@ -25,7 +25,7 @@ LAG = 4
 BIAS_AFTER = 3
 SINGLES_UNTIL = 4
 SINGLES_FROM = 26
-VECTOR_LAST = 4
+VECTOR_LAST = 5
 K_BLOCKS = D // 32
 QUADRANT = 32
 SCALE_ROWS = 4

from contextlib import ExitStack

import concourse.mybir as mybir
from concourse.masks import make_identity

BF16 = mybir.dt.bfloat16
F32 = mybir.dt.float32
I32 = mybir.dt.int32
U32 = mybir.dt.uint32
U8 = mybir.dt.uint8
FP8X4 = mybir.dt.float8_e4m3fn_x4
ACT = mybir.ActivationFunctionType
ALU = mybir.AluOpType

P = 128
PACK = 4
HALVES = 2
BATCH = 4096
D = 512
BLOCKS = BATCH // P
CHUNK = 4
CHUNKS = BLOCKS // CHUNK
PAIR = 2
LAG = 4
BIAS_AFTER = 3
SINGLES_UNTIL = 4
SINGLES_FROM = 26
VECTOR_LAST = 5
K_BLOCKS = D // 32
QUADRANT = 32
SCALE_ROWS = 4
PSUM_BANKS = 8

FLOPS = 4 * 2 * BATCH * D * D


def tile_lstmmirrored_pa_t_kernel(
    tc, x, hist, Wix_words, Wix_scales, Wih_words, Wih_scales, b_i,
    Wcx_words, Wcx_scales, Wch_words, Wch_scales, b_c, out,
):
    nc = tc.nc

    x_blocks = x.rearrange("(p j) k -> p j k", j=BLOCKS)
    h_blocks = hist.rearrange("(p j) k -> p j k", j=BLOCKS)
    out_blocks = out.rearrange("(p j) n -> p j n", j=BLOCKS)

    weight_inputs = (
        (Wix_words, Wix_scales), (Wih_words, Wih_scales),
        (Wcx_words, Wcx_scales), (Wch_words, Wch_scales),
    )
    n_weights = len(weight_inputs)

    with ExitStack() as ctx:
        consts = ctx.enter_context(tc.tile_pool(name="consts", bufs=1))
        sorts = ctx.enter_context(tc.tile_pool(name="sorts", bufs=4))
        stage = ctx.enter_context(tc.tile_pool(name="stage", bufs=8))
        pairs_pool = ctx.enter_context(tc.tile_pool(name="pairs", bufs=6))
        results = ctx.enter_context(tc.tile_pool(name="results", bufs=8))
        psum = ctx.enter_context(tc.psum_pool(name="psum", bufs=PSUM_BANKS))
        ctx.enter_context(tc.manual_schedule())

        w_planes = consts.tile([P, n_weights, D], U8, align_bytes=256)
        nc.vector.memset(w_planes[:].bitcast(I32), 0)
        w_words = consts.tile([P, n_weights, D], U32, align_bytes=256)

        bias_rows = consts.tile([P, 2, D], BF16)
        nc.vector.memset(bias_rows[:], 0.0)
        ones = consts.tile([P, P], BF16)
        nc.vector.memset(ones[:], 1.0)
        nc.scalar.dma_start(out=bias_rows[0:1, 0, :], in_=b_i.rearrange("(o n) -> o n", o=1))
        nc.scalar.dma_start(out=bias_rows[0:1, 1, :], in_=b_c.rearrange("(o n) -> o n", o=1))

        warm = consts.tile([P, 2], F32)
        nc.vector.memset(warm[:], 0.0)
        nc.scalar.activation(out=warm[:, 1:2], in_=warm[:, 0:1], func=ACT.Sigmoid)

        ident = consts.tile([P, P], F32)
        make_identity(nc, ident[:])

        operands = []
        for name, blocks in (("x_rows", x_blocks), ("h_rows", h_blocks)):
            operand_rows = consts.tile([P, BLOCKS, D], BF16, name=name)
            operands.append((operand_rows, blocks))
        scale_turns = list(range(n_weights * SCALE_ROWS))

        def load_scale_rows():
            w, r = divmod(scale_turns.pop(0), SCALE_ROWS)
            scale_rows = weight_inputs[w][1].rearrange("g q n -> (g q) n")
            nc.sync.dma_start(
                out=w_planes[r:P:QUADRANT, w, :].bitcast(I32),
                in_=scale_rows[r:K_BLOCKS:SCALE_ROWS, :].bitcast(I32),
            )

        for c in range(CHUNKS):
            chunk = slice(c * CHUNK, (c + 1) * CHUNK)
            for operand_rows, blocks in operands:
                nc.sync.dma_start(out=operand_rows[:, chunk, :], in_=blocks[:, chunk, :])
                load_scale_rows()
        for w in range(n_weights):
            nc.sync.dma_start(
                out=w_words[:, w, :].bitcast(I32),
                in_=weight_inputs[w][0].rearrange("g p n t -> (g p) (n t)").bitcast(I32),
            )

        codes = consts.tile([P, 2, BLOCKS, P], U32, align_bytes=256)
        planes = consts.tile([P, 2, BLOCKS, P], U8, align_bytes=256)
        waiting = []

        def quantise(leave):
            while len(waiting) > leave:
                grouped, operand, b = waiting.pop(0)
                nc.vector.quantize_mx(
                    out=codes[:, operand, b:b + PAIR, :].rearrange("p j r -> p (j r)").bitcast(FP8X4),
                    scales=planes[:, operand, b:b + PAIR, :].rearrange("p j r -> p (j r)"),
                    in_=grouped[:],
                )

        def sort_words(operand, b):
            words = sorts.tile([P, PAIR, HALVES, P], F32)
            nc.vector.tensor_copy(
                out=words[:],
                in_=operands[operand][0][:, b:b + PAIR, :].rearrange("p j k -> p (j k)").bitcast(F32).rearrange(
                    "p (j w u) -> p j u w", j=PAIR, u=HALVES
                ),
            )
            return words

        def stage_1(operand, b, words):
            flipped = psum.tile([P, PAIR, HALVES, P], F32, tag="bank")
            for j in range(PAIR):
                pairs = operands[operand][0][:, b + j, :].bitcast(F32)
                for u in range(HALVES):
                    if words is None:
                        half = pairs[:, u:D // 2:HALVES]
                    else:
                        half = words[:, j, u, :]
                    nc.tensor.transpose(out=flipped[:, j, u, :], in_=half, identity=ident[:])
            grouped = stage.tile([P, PAIR * P * PACK], BF16, align_bytes=256)
            nc.scalar.copy(
                out=grouped[:].bitcast(F32).rearrange("p (j r u) -> p j r u", j=PAIR, u=HALVES),
                in_=flipped[:].rearrange("p j u r -> p j r u"),
            )
            waiting.append((grouped, operand, b))
            quantise(LAG)

        bias = consts.tile([P, 2, D], F32)

        def spread_biases():
            for gate in range(2):
                spread = psum.tile([P, D], F32, tag="bank")
                nc.tensor.matmul(out=spread[:], lhsT=ones[:], rhs=bias_rows[:, gate, :], start=True, stop=True)
                nc.scalar.copy(out=bias[:, gate, :], in_=spread[:])

        gates = []

        def squash(b):
            if b % PAIR == 0:
                for gate in range(2):
                    squashed = pairs_pool.tile([P, PAIR, D], F32, name="squashed%d" % gate)
                    gates.append(squashed)
            for gate, func in enumerate((ACT.Sigmoid, ACT.Tanh)):
                acc = psum.tile([P, D], F32, tag="bank")
                for operand in range(2):
                    w = 2 * gate + operand
                    nc.tensor.matmul_mx(
                        out=acc[:],
                        lhsT=codes[:, operand, b, :].bitcast(FP8X4),
                        lhsT_scale=planes[:, operand, b, :],
                        rhs=w_words[:, w, :].bitcast(FP8X4),
                        rhs_scale=w_planes[:, w, :],
                        start=(operand == 0),
                        stop=(operand == 1),
                    )
                biased = gates[2 * (b // PAIR) + gate][:, b % PAIR, :]
                nc.vector.tensor_tensor(out=biased, in0=acc[:], in1=bias[:, gate, :], op=ALU.add)
                nc.scalar.activation(out=biased, in_=biased, func=func)

        def multiply(first, count, multiplier, queue):
            halves = slice(first % PAIR, first % PAIR + count)
            result = results.tile([P, PAIR, D], F32)
            multiplier.tensor_tensor(
                out=result[:, halves, :],
                in0=gates[2 * (first // PAIR)][:, halves, :],
                in1=gates[2 * (first // PAIR) + 1][:, halves, :],
                op=ALU.mult,
            )
            queue.dma_start(out=out_blocks[:, first:first + count, :], in_=result[:, halves, :])

        for c in range(CHUNKS):
            for operand in range(2):
                b = c * CHUNK
                words = sort_words(operand, b + PAIR)
                stage_1(operand, b, None)
                stage_1(operand, b + PAIR, words)
            if c == BIAS_AFTER:
                spread_biases()
        quantise(0)
        for b in range(BLOCKS):
            squash(b)
            if b < SINGLES_UNTIL or SINGLES_FROM <= b < BLOCKS - VECTOR_LAST:
                multiply(b, 1, nc.gpsimd, nc.sync)
            elif b % PAIR == PAIR - 1 and b < SINGLES_FROM:
                multiply(b - PAIR + 1, PAIR, nc.gpsimd, nc.sync)
        for b in range(BLOCKS - VECTOR_LAST, BLOCKS):
            multiply(b, 1, nc.vector, nc.scalar)
